import numpy as np
import ml_dtypes


def mxq(x, axis, fmt="e4m3"):
    dtype, down = {"e4m3": (ml_dtypes.float8_e4m3fn, 7), "e5m2": (ml_dtypes.float8_e5m2, 14)}[fmt]
    v = np.moveaxis(np.asarray(x, np.float32).astype(ml_dtypes.bfloat16).astype(np.float64), axis, -1)
    blocks = v.reshape(v.shape[:-1] + (-1, 32))
    amax = np.abs(blocks).max(-1, keepdims=True)
    byte = np.maximum(np.where(amax > 0, np.frexp(amax)[1] - 1 + 127, 0) - down, 1)
    scale = np.exp2(byte - 127.0)
    codes = (blocks / scale).astype(np.float32).astype(dtype).astype(np.float64)
    return np.moveaxis((codes * scale).reshape(v.shape), -1, axis)


WIDE = False


def mx_kscale(k):
    if not WIDE:
        return np.ones(k)
    levels = np.array([10, -10, 5, -5, 0])
    a = np.random.permutation(np.resize(levels, k // 512 * 4)).reshape(k // 512, 4)
    idx = np.arange(k)
    return np.exp2(a[idx // 512, idx % 128 // 32])


BF16 = ml_dtypes.bfloat16


def bf(x):
    return np.asarray(x, np.float32).astype(BF16)


def f64(x):
    return np.asarray(x).astype(np.float64)


B, N, F, H, O = 16, 512, 512, 128, 512
BN_EPS = 1e-3


def setup_inputs():
    s, t = mx_kscale(F), mx_kscale(N)
    return {'x': bf(np.random.standard_normal((B, N, F)) * s / t[:, None]),
            'adj': bf(np.random.uniform(size=(B, N, N)) * (2.0 / N) * t),
            'w': bf(np.random.standard_normal((F, H)) * (0.22 * np.sqrt(N) / np.sqrt(F)) / s[:, None]),
            'bias': bf(np.random.standard_normal(H) * 0.1),
            'gamma': bf(1.0 + 0.1 * np.random.standard_normal(H)),
            'beta': bf(np.random.standard_normal(H) * 0.1),
            'mean': bf(np.random.standard_normal(H) * 0.1),
            'var': bf(0.01 + 0.02 * np.random.uniform(size=H))}


def reference(x, adj, w, bias, gamma, beta, mean, var):
    xw = mxq(f64(x), 2, 'e4m3') @ mxq(f64(w), 0, 'e4m3')
    agg = mxq(f64(adj), 2, 'e4m3') @ mxq(xw, 1, 'e4m3')
    h = np.maximum(agg + f64(bias), 0.0)
    return (h - f64(mean)) * (f64(gamma) / np.sqrt(f64(var) + BN_EPS)) + f64(beta)

@@ -1,0 +1,212 @@
+from contextlib import ExitStack
+
+import concourse.mybir as mybir
+from concourse.masks import make_identity
+
+F32 = mybir.dt.float32
+BF16 = mybir.dt.bfloat16
+U32 = mybir.dt.uint32
+U8 = mybir.dt.uint8
+FP8X4 = mybir.dt.float8_e4m3fn_x4
+ALU = mybir.AluOpType
+
+P = 128
+PACK = 4
+GRAPHS, NODES, FEATURES, HIDDEN = 16, 512, 512, 128
+BN_EPS = 1e-3
+FLOPS = 2 * GRAPHS * NODES * FEATURES * HIDDEN + 2 * GRAPHS * NODES * NODES * HIDDEN
+
+BIAS, GAMMA, BETA, MEAN, VAR = 0, 1, 2, 3, 4
+
+
+def tile_gnn_pa_t_kernel(tc, x, adj, w, bias, gamma, beta, mean, var, out):
+    nc = tc.nc
+    with ExitStack() as stack:
+        stack.enter_context(tc.manual_schedule())
+        const = stack.enter_context(tc.tile_pool(name="const", bufs=1))
+        resident = stack.enter_context(tc.tile_pool(name="resident", bufs=1))
+        work = stack.enter_context(tc.tile_pool(name="work", bufs=2))
+        psum_in = stack.enter_context(tc.psum_pool(name="psum_in", bufs=4))
+        psum_one = stack.enter_context(tc.psum_pool(name="psum_one", bufs=1))
+
+        x_sb = [resident.tile([P, PACK * FEATURES], BF16, name="x%d" % g) for g in range(GRAPHS)]
+        adj_sb = [resident.tile([P, PACK * NODES], BF16, name="adj%d" % g) for g in range(GRAPHS)]
+        for g in range(GRAPHS):
+            nc.sync.dma_start(
+                out=x_sb[g][:].rearrange("p (u r) -> p u r", u=2),
+                in_=x[g].rearrange("(u p e) f -> p u (e f)", u=2, e=2),
+            )
+            nc.sync.dma_start(out=adj_sb[g][:], in_=adj[g].rearrange("(p j) m -> p (j m)", j=PACK))
+
+        w_raw = const.tile([P, PACK, HIDDEN], BF16)
+        nc.scalar.dma_start(
+            out=w_raw[:].rearrange("q (u e) h -> q u (e h)", u=2),
+            in_=w.rearrange("(u q e) h -> q u (e h)", u=2, e=2),
+        )
+        vec_rows = const.tile([P, P], BF16)
+        nc.vector.memset(vec_rows[:], 0.0)
+        for row, vec in ((BIAS, bias), (GAMMA, gamma), (BETA, beta), (MEAN, mean), (VAR, var)):
+            nc.scalar.dma_start(out=vec_rows[row : row + 1, :], in_=vec.rearrange("(o h) -> o h", o=1))
+
+        ident = const.tile([P, P], F32)
+        make_identity(nc, ident[:])
+
+        warm_in = const.tile([P, 1], F32)
+        warm_out = const.tile([P, 1], F32)
+        nc.vector.memset(warm_in[:], 1.0)
+        nc.scalar.sqrt(out=warm_out[:], in_=warm_in[:])
+
+        w_grouped = const.tile([P, HIDDEN, PACK], BF16, align_bytes=64)
+        w_codes = const.tile([P, HIDDEN], U32, align_bytes=64)
+        w_scales = const.tile([P, HIDDEN], U8, align_bytes=64)
+        nc.vector.tensor_copy(out=w_grouped[:], in_=w_raw[:].rearrange("q t h -> q h t"))
+        vec_rows_f32 = const.tile([P, P], F32)
+        nc.vector.tensor_copy(out=vec_rows_f32[:], in_=vec_rows[:])
+        nc.vector.quantize_mx(
+            out=w_codes[:].bitcast(FP8X4), scales=w_scales[:], in_=w_grouped[:].rearrange("q h t -> q (h t)")
+        )
+
+        neg_bias = const.tile([P, 1], F32)
+        gain = const.tile([P, 1], F32)
+        shift_rep = const.tile([P, P], F32)
+        shift_rows = const.tile([P, P], F32)
+
+        def vectors_to_partitions():
+            vec_ps = psum_one.tile([P, P], F32, tag="setup")
+            nc.tensor.transpose(vec_ps[:], vec_rows_f32[:], ident[:])
+            vec_cols = const.tile([P, 8], F32)
+            nc.vector.tensor_copy(out=vec_cols[:], in_=vec_ps[:, 0:8])
+            var_eps = const.tile([P, 1], F32)
+            nc.vector.tensor_scalar_add(out=var_eps[:], in0=vec_cols[:, VAR : VAR + 1], scalar1=BN_EPS)
+            std = const.tile([P, 1], F32)
+            nc.scalar.sqrt(out=std[:], in_=var_eps[:])
+            nc.vector.tensor_scalar_mul(out=neg_bias[:], in0=vec_cols[:, BIAS : BIAS + 1], scalar1=-1.0)
+            centred = const.tile([P, 1], F32)
+            nc.vector.tensor_sub(out=centred[:], in0=vec_cols[:, BIAS : BIAS + 1], in1=vec_cols[:, MEAN : MEAN + 1])
+            inv_std = const.tile([P, 1], F32)
+            nc.vector.reciprocal(out=inv_std[:], in_=std[:])
+            nc.vector.tensor_mul(out=gain[:], in0=vec_cols[:, GAMMA : GAMMA + 1], in1=inv_std[:])
+            shift = const.tile([P, 1], F32)
+            nc.vector.tensor_scalar(
+                out=shift[:], in0=centred[:], scalar1=gain[:, 0:1], scalar2=vec_cols[:, BETA : BETA + 1],
+                op0=ALU.mult, op1=ALU.add,
+            )
+            nc.vector.tensor_copy(out=shift_rep[:], in_=shift[:, 0:1].to_broadcast([P, P]))
+
+        def shift_to_rows():
+            shift_ps = psum_one.tile([P, P], F32, tag="setup")
+            nc.tensor.transpose(shift_ps[:], shift_rep[:], ident[:])
+            nc.vector.tensor_copy(out=shift_rows[:], in_=shift_ps[:])
+
+        grouped = {}
+        quantised = {}
+        scaled = {}
+        result_ps = {}
+
+        def transpose_operand(name, g, rows_sb):
+            words = rows_sb[:].bitcast(F32)
+            tile_g = work.tile([P, PACK * 512], BF16, tag="%s_grouped" % name, name="%s_grouped" % name, align_bytes=64)
+            grouped_words = tile_g[:].bitcast(F32)
+            for pair in range(2):
+                bank = psum_in.tile([P, 2, 2 * P], F32, tag="bank", name="bank")
+                for half in range(2):
+                    for s in range(2):
+                        first = 256 * (2 * pair + s) + P * half
+                        nc.tensor.transpose(bank[:, half, P * s : P * (s + 1)], words[:, first : first + P], ident[:])
+                nc.scalar.copy(
+                    out=grouped_words[:, 512 * pair : 512 * (pair + 1)].rearrange("q (c half) -> q c half", half=2),
+                    in_=bank[:].rearrange("q half c -> q c half"),
+                )
+            grouped[(name, g)] = tile_g
+
+        def quantise(name, g, columns):
+            codes = work.tile([P, columns], U32, tag="%s_codes" % name, name="%s_codes" % name, align_bytes=64)
+            scales = work.tile([P, columns], U8, tag="%s_scales" % name, name="%s_scales" % name, align_bytes=64)
+            nc.vector.quantize_mx(out=codes[:].bitcast(FP8X4), scales=scales[:], in_=grouped[(name, g)][:])
+            quantised[(name, g)] = (codes, scales)
+
+        def first_product(g):
+            x_codes, x_scales = quantised[("x", g)]
+            xw_ps = psum_one.tile([P, PACK, HIDDEN], F32, tag="xw_ps")
+            for t in range(PACK):
+                nc.tensor.matmul_mx(
+                    out=xw_ps[:, t, :],
+                    lhsT=x_codes[:, P * t : P * (t + 1)].bitcast(FP8X4),
+                    lhsT_scale=x_scales[:, P * t : P * (t + 1)],
+                    rhs=w_codes[:].bitcast(FP8X4),
+                    rhs_scale=w_scales[:],
+                    start=True,
+                    stop=True,
+                )
+            xw_grouped = work.tile([P, HIDDEN * PACK], BF16, tag="xw_grouped", align_bytes=64)
+            nc.scalar.copy(
+                out=xw_grouped[:].rearrange("p (h t) -> p h t", t=PACK), in_=xw_ps[:].rearrange("p t h -> p h t")
+            )
+            grouped[("xw", g)] = xw_grouped
+
+        def second_product(g):
+            xw_codes, xw_scales = quantised[("xw", g)]
+            adj_codes, adj_scales = quantised[("adj", g)]
+            agg_ps = psum_one.tile([P, NODES], F32, tag="agg_ps")
+            nc.tensor.matmul_mx(
+                out=agg_ps[:],
+                lhsT=xw_codes[:].bitcast(FP8X4),
+                lhsT_scale=xw_scales[:],
+                rhs=adj_codes[:].bitcast(FP8X4),
+                rhs_scale=adj_scales[:],
+                start=True,
+                stop=True,
+            )
+            return agg_ps
+
+        def relu_and_gain(g, agg_ps):
+            scaled_sb = work.tile([P, NODES], F32, tag="scaled")
+            nc.vector.tensor_scalar(
+                out=scaled_sb[:], in0=agg_ps[:], scalar1=neg_bias[:, 0:1], scalar2=gain[:, 0:1],
+                op0=ALU.max, op1=ALU.mult,
+            )
+            scaled[g] = scaled_sb
+
+        def transpose_result(g):
+            res_ps = psum_one.tile([P, PACK, HIDDEN], F32, tag="res_ps")
+            for j in range(PACK):
+                nc.tensor.transpose(res_ps[:, j, :], scaled[g][:, P * j : P * (j + 1)], ident[:])
+            result_ps[g] = res_ps
+
+        def shift_and_store(g):
+            res_sb = resident.tile([P, PACK, HIDDEN], F32, name="res%d" % g)
+            nc.vector.tensor_tensor(
+                out=res_sb[:], in0=result_ps[g][:], in1=shift_rows[:].unsqueeze(1).to_broadcast([P, PACK, HIDDEN]),
+                op=ALU.add,
+            )
+            nc.sync.dma_start(
+                out=out[g].rearrange("(p j) h -> p (j h)", j=PACK), in_=res_sb[:].rearrange("p j h -> p (j h)")
+            )
+
+        def is_graph(g):
+            return 0 <= g < GRAPHS
+
+        for r in range(GRAPHS + 3):
+            if is_graph(r):
+                transpose_operand("x", r, x_sb[r])
+                transpose_operand("adj", r, adj_sb[r])
+            if is_graph(r - 3):
+                transpose_result(r - 3)
+            if r == 2:
+                shift_to_rows()
+            if is_graph(r - 1):
+                quantise("adj", r - 1, NODES)
+            if is_graph(r - 2):
+                quantise("xw", r - 2, HIDDEN)
+            if is_graph(r - 1):
+                first_product(r - 1)
+            if is_graph(r - 2):
+                agg_ps = second_product(r - 2)
+            if is_graph(r):
+                quantise("x", r, NODES)
+            if is_graph(r - 3):
+                shift_and_store(r - 3)
+            if is_graph(r - 2):
+                relu_and_gain(r - 2, agg_ps)
+            if r == 0:
+                vectors_to_partitions()

@@ -16,6 +16,8 @@ GRAPHS, NODES, FEATURES, HIDDEN = 16, 512, 512, 128
 BN_EPS = 1e-3
 FLOPS = 2 * GRAPHS * NODES * FEATURES * HIDDEN + 2 * GRAPHS * NODES * NODES * HIDDEN
 
+VECTOR_HELPS_EVERY = 4
+
 BIAS, GAMMA, BETA, MEAN, VAR = 0, 1, 2, 3, 4
 
 
@@ -29,13 +31,13 @@ def tile_gnn_pa_t_kernel(tc, x, adj, w, bias, gamma, beta, mean, var, out):
         psum_in = stack.enter_context(tc.psum_pool(name="psum_in", bufs=4))
         psum_one = stack.enter_context(tc.psum_pool(name="psum_one", bufs=1))
 
-        x_sb = [resident.tile([P, PACK * FEATURES], BF16, name="x%d" % g) for g in range(GRAPHS)]
+        x_sb = [[resident.tile([P, 2 * FEATURES], BF16, name="x%d_%d" % (g, u)) for u in range(2)] for g in range(GRAPHS)]
         adj_sb = [resident.tile([P, PACK * NODES], BF16, name="adj%d" % g) for g in range(GRAPHS)]
         for g in range(GRAPHS):
-            nc.sync.dma_start(
-                out=x_sb[g][:].rearrange("p (u r) -> p u r", u=2),
-                in_=x[g].rearrange("(u p e) f -> p u (e f)", u=2, e=2),
-            )
+            for u in range(2):
+                nc.sync.dma_start(
+                    out=x_sb[g][u][:], in_=x[g, 256 * u : 256 * (u + 1), :].rearrange("(p e) f -> p (e f)", e=2)
+                )
             nc.sync.dma_start(out=adj_sb[g][:], in_=adj[g].rearrange("(p j) m -> p (j m)", j=PACK))
 
         w_raw = const.tile([P, PACK, HIDDEN], BF16)
@@ -60,8 +62,6 @@ def tile_gnn_pa_t_kernel(tc, x, adj, w, bias, gamma, beta, mean, var, out):
         w_codes = const.tile([P, HIDDEN], U32, align_bytes=64)
         w_scales = const.tile([P, HIDDEN], U8, align_bytes=64)
         nc.vector.tensor_copy(out=w_grouped[:], in_=w_raw[:].rearrange("q t h -> q h t"))
-        vec_rows_f32 = const.tile([P, P], F32)
-        nc.vector.tensor_copy(out=vec_rows_f32[:], in_=vec_rows[:])
         nc.vector.quantize_mx(
             out=w_codes[:].bitcast(FP8X4), scales=w_scales[:], in_=w_grouped[:].rearrange("q h t -> q (h t)")
         )
@@ -72,6 +72,8 @@ def tile_gnn_pa_t_kernel(tc, x, adj, w, bias, gamma, beta, mean, var, out):
         shift_rows = const.tile([P, P], F32)
 
         def vectors_to_partitions():
+            vec_rows_f32 = const.tile([P, P], F32)
+            nc.vector.tensor_copy(out=vec_rows_f32[:], in_=vec_rows[:])
             vec_ps = psum_one.tile([P, P], F32, tag="setup")
             nc.tensor.transpose(vec_ps[:], vec_rows_f32[:], ident[:])
             vec_cols = const.tile([P, 8], F32)
@@ -103,20 +105,22 @@ def tile_gnn_pa_t_kernel(tc, x, adj, w, bias, gamma, beta, mean, var, out):
         scaled = {}
         result_ps = {}
 
-        def transpose_operand(name, g, rows_sb):
-            words = rows_sb[:].bitcast(F32)
+        def transpose_operand(name, g, slot_pairs, vector_helps):
             tile_g = work.tile([P, PACK * 512], BF16, tag="%s_grouped" % name, name="%s_grouped" % name, align_bytes=64)
             grouped_words = tile_g[:].bitcast(F32)
             for pair in range(2):
                 bank = psum_in.tile([P, 2, 2 * P], F32, tag="bank", name="bank")
                 for half in range(2):
                     for s in range(2):
-                        first = 256 * (2 * pair + s) + P * half
-                        nc.tensor.transpose(bank[:, half, P * s : P * (s + 1)], words[:, first : first + P], ident[:])
-                nc.scalar.copy(
-                    out=grouped_words[:, 512 * pair : 512 * (pair + 1)].rearrange("q (c half) -> q c half", half=2),
-                    in_=bank[:].rearrange("q half c -> q c half"),
-                )
+                        first = 256 * s + P * half
+                        nc.tensor.transpose(
+                            bank[:, half, P * s : P * (s + 1)], slot_pairs[pair][:, first : first + P], ident[:]
+                        )
+                interleaved = grouped_words[:, 512 * pair : 512 * (pair + 1)].rearrange("q (c half) -> q c half", half=2)
+                if vector_helps and pair == 1:
+                    nc.vector.tensor_copy(out=interleaved, in_=bank[:].rearrange("q half c -> q c half"))
+                else:
+                    nc.scalar.copy(out=interleaved, in_=bank[:].rearrange("q half c -> q c half"))
             grouped[(name, g)] = tile_g
 
         def quantise(name, g, columns):
@@ -188,8 +192,9 @@ def tile_gnn_pa_t_kernel(tc, x, adj, w, bias, gamma, beta, mean, var, out):
 
         for r in range(GRAPHS + 3):
             if is_graph(r):
-                transpose_operand("x", r, x_sb[r])
-                transpose_operand("adj", r, adj_sb[r])
+                transpose_operand("x", r, [half[:].bitcast(F32) for half in x_sb[r]], r % VECTOR_HELPS_EVERY == 0)
+                adj_words = adj_sb[r][:].bitcast(F32)
+                transpose_operand("adj", r, [adj_words[:, 0:512], adj_words[:, 512:1024]], False)
             if is_graph(r - 3):
                 transpose_result(r - 3)
             if r == 2:
@@ -202,10 +207,10 @@ def tile_gnn_pa_t_kernel(tc, x, adj, w, bias, gamma, beta, mean, var, out):
                 first_product(r - 1)
             if is_graph(r - 2):
                 agg_ps = second_product(r - 2)
-            if is_graph(r):
-                quantise("x", r, NODES)
             if is_graph(r - 3):
                 shift_and_store(r - 3)
+            if is_graph(r):
+                quantise("x", r, NODES)
             if is_graph(r - 2):
                 relu_and_gain(r - 2, agg_ps)
             if r == 0:

@@ -16,8 +16,6 @@ GRAPHS, NODES, FEATURES, HIDDEN = 16, 512, 512, 128
 BN_EPS = 1e-3
 FLOPS = 2 * GRAPHS * NODES * FEATURES * HIDDEN + 2 * GRAPHS * NODES * NODES * HIDDEN
 
-VECTOR_HELPS_EVERY = 4
-
 BIAS, GAMMA, BETA, MEAN, VAR = 0, 1, 2, 3, 4
 
 
@@ -31,13 +29,13 @@ def tile_gnn_pa_t_kernel(tc, x, adj, w, bias, gamma, beta, mean, var, out):
         psum_in = stack.enter_context(tc.psum_pool(name="psum_in", bufs=4))
         psum_one = stack.enter_context(tc.psum_pool(name="psum_one", bufs=1))
 
-        x_sb = [[resident.tile([P, 2 * FEATURES], BF16, name="x%d_%d" % (g, u)) for u in range(2)] for g in range(GRAPHS)]
+        x_sb = [resident.tile([P, PACK * FEATURES], BF16, name="x%d" % g) for g in range(GRAPHS)]
         adj_sb = [resident.tile([P, PACK * NODES], BF16, name="adj%d" % g) for g in range(GRAPHS)]
         for g in range(GRAPHS):
-            for u in range(2):
-                nc.sync.dma_start(
-                    out=x_sb[g][u][:], in_=x[g, 256 * u : 256 * (u + 1), :].rearrange("(p e) f -> p (e f)", e=2)
-                )
+            nc.sync.dma_start(
+                out=x_sb[g][:].rearrange("p (u r) -> p u r", u=2),
+                in_=x[g].rearrange("(u p e) f -> p u (e f)", u=2, e=2),
+            )
             nc.sync.dma_start(out=adj_sb[g][:], in_=adj[g].rearrange("(p j) m -> p (j m)", j=PACK))
 
         w_raw = const.tile([P, PACK, HIDDEN], BF16)
@@ -62,6 +60,8 @@ def tile_gnn_pa_t_kernel(tc, x, adj, w, bias, gamma, beta, mean, var, out):
         w_codes = const.tile([P, HIDDEN], U32, align_bytes=64)
         w_scales = const.tile([P, HIDDEN], U8, align_bytes=64)
         nc.vector.tensor_copy(out=w_grouped[:], in_=w_raw[:].rearrange("q t h -> q h t"))
+        vec_rows_f32 = const.tile([P, P], F32)
+        nc.vector.tensor_copy(out=vec_rows_f32[:], in_=vec_rows[:])
         nc.vector.quantize_mx(
             out=w_codes[:].bitcast(FP8X4), scales=w_scales[:], in_=w_grouped[:].rearrange("q h t -> q (h t)")
         )
@@ -72,8 +72,6 @@ def tile_gnn_pa_t_kernel(tc, x, adj, w, bias, gamma, beta, mean, var, out):
         shift_rows = const.tile([P, P], F32)
 
         def vectors_to_partitions():
-            vec_rows_f32 = const.tile([P, P], F32)
-            nc.vector.tensor_copy(out=vec_rows_f32[:], in_=vec_rows[:])
             vec_ps = psum_one.tile([P, P], F32, tag="setup")
             nc.tensor.transpose(vec_ps[:], vec_rows_f32[:], ident[:])
             vec_cols = const.tile([P, 8], F32)
@@ -105,22 +103,20 @@ def tile_gnn_pa_t_kernel(tc, x, adj, w, bias, gamma, beta, mean, var, out):
         scaled = {}
         result_ps = {}
 
-        def transpose_operand(name, g, slot_pairs, vector_helps):
+        def transpose_operand(name, g, rows_sb):
+            words = rows_sb[:].bitcast(F32)
             tile_g = work.tile([P, PACK * 512], BF16, tag="%s_grouped" % name, name="%s_grouped" % name, align_bytes=64)
             grouped_words = tile_g[:].bitcast(F32)
             for pair in range(2):
                 bank = psum_in.tile([P, 2, 2 * P], F32, tag="bank", name="bank")
                 for half in range(2):
                     for s in range(2):
-                        first = 256 * s + P * half
-                        nc.tensor.transpose(
-                            bank[:, half, P * s : P * (s + 1)], slot_pairs[pair][:, first : first + P], ident[:]
-                        )
-                interleaved = grouped_words[:, 512 * pair : 512 * (pair + 1)].rearrange("q (c half) -> q c half", half=2)
-                if vector_helps and pair == 1:
-                    nc.vector.tensor_copy(out=interleaved, in_=bank[:].rearrange("q half c -> q c half"))
-                else:
-                    nc.scalar.copy(out=interleaved, in_=bank[:].rearrange("q half c -> q c half"))
+                        first = 256 * (2 * pair + s) + P * half
+                        nc.tensor.transpose(bank[:, half, P * s : P * (s + 1)], words[:, first : first + P], ident[:])
+                nc.scalar.copy(
+                    out=grouped_words[:, 512 * pair : 512 * (pair + 1)].rearrange("q (c half) -> q c half", half=2),
+                    in_=bank[:].rearrange("q half c -> q c half"),
+                )
             grouped[(name, g)] = tile_g
 
         def quantise(name, g, columns):
@@ -161,6 +157,16 @@ def tile_gnn_pa_t_kernel(tc, x, adj, w, bias, gamma, beta, mean, var, out):
                 start=True,
                 stop=True,
             )
+            spare_ps = psum_one.tile([P, NODES], F32, tag="setup")
+            nc.tensor.matmul_mx(
+                out=spare_ps[:],
+                lhsT=xw_codes[:].bitcast(FP8X4),
+                lhsT_scale=xw_scales[:],
+                rhs=adj_codes[:].bitcast(FP8X4),
+                rhs_scale=adj_scales[:],
+                start=True,
+                stop=True,
+            )
             return agg_ps
 
         def relu_and_gain(g, agg_ps):
@@ -192,9 +198,8 @@ def tile_gnn_pa_t_kernel(tc, x, adj, w, bias, gamma, beta, mean, var, out):
 
         for r in range(GRAPHS + 3):
             if is_graph(r):
-                transpose_operand("x", r, [half[:].bitcast(F32) for half in x_sb[r]], r % VECTOR_HELPS_EVERY == 0)
-                adj_words = adj_sb[r][:].bitcast(F32)
-                transpose_operand("adj", r, [adj_words[:, 0:512], adj_words[:, 512:1024]], False)
+                transpose_operand("x", r, x_sb[r])
+                transpose_operand("adj", r, adj_sb[r])
             if is_graph(r - 3):
                 transpose_result(r - 3)
             if r == 2:
@@ -207,10 +212,10 @@ def tile_gnn_pa_t_kernel(tc, x, adj, w, bias, gamma, beta, mean, var, out):
                 first_product(r - 1)
             if is_graph(r - 2):
                 agg_ps = second_product(r - 2)
-            if is_graph(r - 3):
-                shift_and_store(r - 3)
             if is_graph(r):
                 quantise("x", r, NODES)
+            if is_graph(r - 3):
+                shift_and_store(r - 3)
             if is_graph(r - 2):
                 relu_and_gain(r - 2, agg_ps)
             if r == 0:

from contextlib import ExitStack

import concourse.mybir as mybir
from concourse.masks import make_identity

F32 = mybir.dt.float32
BF16 = mybir.dt.bfloat16
U32 = mybir.dt.uint32
U8 = mybir.dt.uint8
FP8X4 = mybir.dt.float8_e4m3fn_x4
ALU = mybir.AluOpType

P = 128
PACK = 4
GRAPHS, NODES, FEATURES, HIDDEN = 16, 512, 512, 128
BN_EPS = 1e-3
FLOPS = 2 * GRAPHS * NODES * FEATURES * HIDDEN + 2 * GRAPHS * NODES * NODES * HIDDEN

BIAS, GAMMA, BETA, MEAN, VAR = 0, 1, 2, 3, 4


def tile_gnn_pa_t_kernel(tc, x, adj, w, bias, gamma, beta, mean, var, out):
    nc = tc.nc
    with ExitStack() as stack:
        stack.enter_context(tc.manual_schedule())
        const = stack.enter_context(tc.tile_pool(name="const", bufs=1))
        resident = stack.enter_context(tc.tile_pool(name="resident", bufs=1))
        work = stack.enter_context(tc.tile_pool(name="work", bufs=2))
        psum_in = stack.enter_context(tc.psum_pool(name="psum_in", bufs=4))
        psum_one = stack.enter_context(tc.psum_pool(name="psum_one", bufs=1))

        x_sb = [resident.tile([P, PACK * FEATURES], BF16, name="x%d" % g) for g in range(GRAPHS)]
        adj_sb = [resident.tile([P, PACK * NODES], BF16, name="adj%d" % g) for g in range(GRAPHS)]
        for g in range(GRAPHS):
            nc.sync.dma_start(
                out=x_sb[g][:].rearrange("p (u r) -> p u r", u=2),
                in_=x[g].rearrange("(u p e) f -> p u (e f)", u=2, e=2),
            )
            nc.sync.dma_start(out=adj_sb[g][:], in_=adj[g].rearrange("(p j) m -> p (j m)", j=PACK))

        w_raw = const.tile([P, PACK, HIDDEN], BF16)
        nc.scalar.dma_start(
            out=w_raw[:].rearrange("q (u e) h -> q u (e h)", u=2),
            in_=w.rearrange("(u q e) h -> q u (e h)", u=2, e=2),
        )
        vec_rows = const.tile([P, P], BF16)
        nc.vector.memset(vec_rows[:], 0.0)
        for row, vec in ((BIAS, bias), (GAMMA, gamma), (BETA, beta), (MEAN, mean), (VAR, var)):
            nc.scalar.dma_start(out=vec_rows[row : row + 1, :], in_=vec.rearrange("(o h) -> o h", o=1))

        ident = const.tile([P, P], F32)
        make_identity(nc, ident[:])

        warm_in = const.tile([P, 1], F32)
        warm_out = const.tile([P, 1], F32)
        nc.vector.memset(warm_in[:], 1.0)
        nc.scalar.sqrt(out=warm_out[:], in_=warm_in[:])

        w_grouped = const.tile([P, HIDDEN, PACK], BF16, align_bytes=64)
        w_codes = const.tile([P, HIDDEN], U32, align_bytes=64)
        w_scales = const.tile([P, HIDDEN], U8, align_bytes=64)
        nc.vector.tensor_copy(out=w_grouped[:], in_=w_raw[:].rearrange("q t h -> q h t"))
        vec_rows_f32 = const.tile([P, P], F32)
        nc.vector.tensor_copy(out=vec_rows_f32[:], in_=vec_rows[:])
        nc.vector.quantize_mx(
            out=w_codes[:].bitcast(FP8X4), scales=w_scales[:], in_=w_grouped[:].rearrange("q h t -> q (h t)")
        )

        neg_bias = const.tile([P, 1], F32)
        gain = const.tile([P, 1], F32)
        shift_rep = const.tile([P, P], F32)
        shift_rows = const.tile([P, P], F32)

        def vectors_to_partitions():
            vec_ps = psum_one.tile([P, P], F32, tag="setup")
            nc.tensor.transpose(vec_ps[:], vec_rows_f32[:], ident[:])
            vec_cols = const.tile([P, 8], F32)
            nc.vector.tensor_copy(out=vec_cols[:], in_=vec_ps[:, 0:8])
            var_eps = const.tile([P, 1], F32)
            nc.vector.tensor_scalar_add(out=var_eps[:], in0=vec_cols[:, VAR : VAR + 1], scalar1=BN_EPS)
            std = const.tile([P, 1], F32)
            nc.scalar.sqrt(out=std[:], in_=var_eps[:])
            nc.vector.tensor_scalar_mul(out=neg_bias[:], in0=vec_cols[:, BIAS : BIAS + 1], scalar1=-1.0)
            centred = const.tile([P, 1], F32)
            nc.vector.tensor_sub(out=centred[:], in0=vec_cols[:, BIAS : BIAS + 1], in1=vec_cols[:, MEAN : MEAN + 1])
            inv_std = const.tile([P, 1], F32)
            nc.vector.reciprocal(out=inv_std[:], in_=std[:])
            nc.vector.tensor_mul(out=gain[:], in0=vec_cols[:, GAMMA : GAMMA + 1], in1=inv_std[:])
            shift = const.tile([P, 1], F32)
            nc.vector.tensor_scalar(
                out=shift[:], in0=centred[:], scalar1=gain[:, 0:1], scalar2=vec_cols[:, BETA : BETA + 1],
                op0=ALU.mult, op1=ALU.add,
            )
            nc.vector.tensor_copy(out=shift_rep[:], in_=shift[:, 0:1].to_broadcast([P, P]))

        def shift_to_rows():
            shift_ps = psum_one.tile([P, P], F32, tag="setup")
            nc.tensor.transpose(shift_ps[:], shift_rep[:], ident[:])
            nc.vector.tensor_copy(out=shift_rows[:], in_=shift_ps[:])

        grouped = {}
        quantised = {}
        scaled = {}
        result_ps = {}

        def transpose_operand(name, g, rows_sb):
            words = rows_sb[:].bitcast(F32)
            tile_g = work.tile([P, PACK * 512], BF16, tag="%s_grouped" % name, name="%s_grouped" % name, align_bytes=64)
            grouped_words = tile_g[:].bitcast(F32)
            for pair in range(2):
                bank = psum_in.tile([P, 2, 2 * P], F32, tag="bank", name="bank")
                for half in range(2):
                    for s in range(2):
                        first = 256 * (2 * pair + s) + P * half
                        nc.tensor.transpose(bank[:, half, P * s : P * (s + 1)], words[:, first : first + P], ident[:])
                nc.scalar.copy(
                    out=grouped_words[:, 512 * pair : 512 * (pair + 1)].rearrange("q (c half) -> q c half", half=2),
                    in_=bank[:].rearrange("q half c -> q c half"),
                )
            grouped[(name, g)] = tile_g

        def quantise(name, g, columns):
            codes = work.tile([P, columns], U32, tag="%s_codes" % name, name="%s_codes" % name, align_bytes=64)
            scales = work.tile([P, columns], U8, tag="%s_scales" % name, name="%s_scales" % name, align_bytes=64)
            nc.vector.quantize_mx(out=codes[:].bitcast(FP8X4), scales=scales[:], in_=grouped[(name, g)][:])
            quantised[(name, g)] = (codes, scales)

        def first_product(g):
            x_codes, x_scales = quantised[("x", g)]
            xw_ps = psum_one.tile([P, PACK, HIDDEN], F32, tag="xw_ps")
            for t in range(PACK):
                nc.tensor.matmul_mx(
                    out=xw_ps[:, t, :],
                    lhsT=x_codes[:, P * t : P * (t + 1)].bitcast(FP8X4),
                    lhsT_scale=x_scales[:, P * t : P * (t + 1)],
                    rhs=w_codes[:].bitcast(FP8X4),
                    rhs_scale=w_scales[:],
                    start=True,
                    stop=True,
                )
            xw_grouped = work.tile([P, HIDDEN * PACK], BF16, tag="xw_grouped", align_bytes=64)
            nc.scalar.copy(
                out=xw_grouped[:].rearrange("p (h t) -> p h t", t=PACK), in_=xw_ps[:].rearrange("p t h -> p h t")
            )
            grouped[("xw", g)] = xw_grouped

        def second_product(g):
            xw_codes, xw_scales = quantised[("xw", g)]
            adj_codes, adj_scales = quantised[("adj", g)]
            agg_ps = psum_one.tile([P, NODES], F32, tag="agg_ps")
            nc.tensor.matmul_mx(
                out=agg_ps[:],
                lhsT=xw_codes[:].bitcast(FP8X4),
                lhsT_scale=xw_scales[:],
                rhs=adj_codes[:].bitcast(FP8X4),
                rhs_scale=adj_scales[:],
                start=True,
                stop=True,
            )
            spare_ps = psum_one.tile([P, NODES], F32, tag="setup")
            nc.tensor.matmul_mx(
                out=spare_ps[:],
                lhsT=xw_codes[:].bitcast(FP8X4),
                lhsT_scale=xw_scales[:],
                rhs=adj_codes[:].bitcast(FP8X4),
                rhs_scale=adj_scales[:],
                start=True,
                stop=True,
            )
            return agg_ps

        def relu_and_gain(g, agg_ps):
            scaled_sb = work.tile([P, NODES], F32, tag="scaled")
            nc.vector.tensor_scalar(
                out=scaled_sb[:], in0=agg_ps[:], scalar1=neg_bias[:, 0:1], scalar2=gain[:, 0:1],
                op0=ALU.max, op1=ALU.mult,
            )
            scaled[g] = scaled_sb

        def transpose_result(g):
            res_ps = psum_one.tile([P, PACK, HIDDEN], F32, tag="res_ps")
            for j in range(PACK):
                nc.tensor.transpose(res_ps[:, j, :], scaled[g][:, P * j : P * (j + 1)], ident[:])
            result_ps[g] = res_ps

        def shift_and_store(g):
            res_sb = resident.tile([P, PACK, HIDDEN], F32, name="res%d" % g)
            nc.vector.tensor_tensor(
                out=res_sb[:], in0=result_ps[g][:], in1=shift_rows[:].unsqueeze(1).to_broadcast([P, PACK, HIDDEN]),
                op=ALU.add,
            )
            nc.sync.dma_start(
                out=out[g].rearrange("(p j) h -> p (j h)", j=PACK), in_=res_sb[:].rearrange("p j h -> p (j h)")
            )

        def is_graph(g):
            return 0 <= g < GRAPHS

        for r in range(GRAPHS + 3):
            if is_graph(r):
                transpose_operand("x", r, x_sb[r])
                transpose_operand("adj", r, adj_sb[r])
            if is_graph(r - 3):
                transpose_result(r - 3)
            if r == 2:
                shift_to_rows()
            if is_graph(r - 1):
                quantise("adj", r - 1, NODES)
            if is_graph(r - 2):
                quantise("xw", r - 2, HIDDEN)
            if is_graph(r - 1):
                first_product(r - 1)
            if is_graph(r - 2):
                agg_ps = second_product(r - 2)
            if is_graph(r):
                quantise("x", r, NODES)
            if is_graph(r - 3):
                shift_and_store(r - 3)
            if is_graph(r - 2):
                relu_and_gain(r - 2, agg_ps)
            if r == 0:
                vectors_to_partitions()
